import numpy as np
import ml_dtypes


def mxq(x, axis, fmt="e4m3"):
    dtype, down = {"e4m3": (ml_dtypes.float8_e4m3fn, 7), "e5m2": (ml_dtypes.float8_e5m2, 14)}[fmt]
    v = np.moveaxis(np.asarray(x, np.float32).astype(ml_dtypes.bfloat16).astype(np.float64), axis, -1)
    blocks = v.reshape(v.shape[:-1] + (-1, 32))
    amax = np.abs(blocks).max(-1, keepdims=True)
    byte = np.maximum(np.where(amax > 0, np.frexp(amax)[1] - 1 + 127, 0) - down, 1)
    scale = np.exp2(byte - 127.0)
    codes = (blocks / scale).astype(np.float32).astype(dtype).astype(np.float64)
    return np.moveaxis((codes * scale).reshape(v.shape), -1, axis)


WIDE = False


def mx_kscale(k):
    if not WIDE:
        return np.ones(k)
    levels = np.array([10, -10, 5, -5, 0])
    a = np.random.permutation(np.resize(levels, k // 512 * 4)).reshape(k // 512, 4)
    idx = np.arange(k)
    return np.exp2(a[idx // 512, idx % 128 // 32])


BF16 = ml_dtypes.bfloat16


def bf(x):
    return np.asarray(x, np.float32).astype(BF16)


def f64(x):
    return np.asarray(x).astype(np.float64)


N, C, H, W, HIDDEN, OUT = 8, 512, 16, 16, 512, 256
P = H * W
M = N * P


def leaky_relu(v):
    return np.where(v >= 0.0, v, 0.01 * v)


def setup_inputs():
    s, t = mx_kscale(M), mx_kscale(C)
    strong = np.where(np.random.random((M, M)) * N < 1.0, 1.0, 0.02)
    weight = np.random.random((M, M)) * strong * 2.0 / P
    x = np.random.standard_normal((N, C, H, W)) * 0.25 * np.sqrt(P)
    return {"x": bf(x * t[None, :, None, None] / s.reshape(N, 1, H, W)),
            "weight": bf(weight * s[None, :]),
            "W1": bf(np.random.standard_normal((HIDDEN, C)) * 3.0 / np.sqrt(C) / t[None, :]),
            "b1": bf(np.random.standard_normal(HIDDEN) * 0.2 - 0.4)}


def reference(x, weight, W1, b1):
    nodes = f64(x).transpose(0, 2, 3, 1).reshape(-1, C)
    agg = mxq(f64(weight), 1, "e4m3") @ mxq(nodes, 0, "e4m3")
    return leaky_relu((mxq(agg, 1, "e4m3") @ mxq(f64(W1), 1, "e4m3").T) + f64(b1))

@@ -1,0 +1,192 @@
+from contextlib import ExitStack
+
+import concourse.mybir as mybir
+from concourse.masks import make_identity
+
+F32 = mybir.dt.float32
+BF16 = mybir.dt.bfloat16
+U32 = mybir.dt.uint32
+U8 = mybir.dt.uint8
+FP8X4 = mybir.dt.float8_e4m3fn_x4
+ALU = mybir.AluOpType
+
+P = 128
+PACK = 4
+K_PASS = P * PACK
+BANK = 512
+BANKS = 8
+
+SAMPLES, CHANNELS, PIXELS = 8, 512, 256
+NODES = SAMPLES * PIXELS
+HIDDEN = 512
+SLOPE = 0.01
+
+PASSES = NODES // K_PASS
+GROUPS = CHANNELS // P
+TILES = 2
+ROUNDS = NODES // (TILES * P)
+TILE_WORDS = NODES // 2
+
+FLOPS = 2 * NODES * NODES * CHANNELS + 2 * NODES * CHANNELS * HIDDEN
+
+
+def tile_similargcn_pa_kernel(tc, x, weight, W1, b1, out):
+    nc = tc.nc
+    with ExitStack() as ctx:
+        keep = ctx.enter_context(tc.tile_pool(name="keep", bufs=1))
+        raw = ctx.enter_context(tc.tile_pool(name="raw", bufs=ROUNDS))
+        work = ctx.enter_context(tc.tile_pool(name="work", bufs=3))
+        psum = ctx.enter_context(tc.psum_pool(name="psum", bufs=BANKS))
+        ctx.enter_context(tc.manual_schedule())
+
+        ident = keep.tile([P, P], F32)
+        make_identity(nc, ident[:])
+        ones = keep.tile([P, P], BF16)
+        nc.gpsimd.memset(ones[:], 1.0)
+        bias_rows = keep.tile([P, HIDDEN], BF16)
+        nc.gpsimd.memset(bias_rows[:], 0.0)
+
+        x_view = x.rearrange("n (p j) h w -> p n (j h w)", j=GROUPS)
+        x_raw = keep.tile([P, SAMPLES * GROUPS * PIXELS], BF16)
+        x_raw_by_sample = x_raw[:].rearrange("p (n f) -> p n f", n=SAMPLES)
+        for g in range(PASSES):
+            nc.sync.dma_start(out=x_raw_by_sample[:, 2 * g : 2 * g + 2, :], in_=x_view[:, 2 * g : 2 * g + 2, :])
+        weight_rounds = weight.rearrange("(i p r) k -> i p (r k)", p=P, r=TILES)
+        out_rounds = out.rearrange("(i p r) h -> i p (r h)", p=P, r=TILES)
+        w1_raw = keep.tile([P, GROUPS * CHANNELS], BF16)
+        w_raws = []
+        for i in range(ROUNDS):
+            w_raw = raw.tile([P, TILES * NODES], BF16)
+            nc.sync.dma_start(out=w_raw[:], in_=weight_rounds[i])
+            w_raws.append(w_raw)
+            if i == 0:
+                nc.sync.dma_start(
+                    out=w1_raw[:].rearrange("p (a c) -> p a c", a=GROUPS),
+                    in_=W1.rearrange("(a p) c -> p a c", p=P),
+                )
+                nc.sync.dma_start(out=bias_rows[0:1, :], in_=b1.rearrange("(o h) -> o h", o=1))
+
+        def transpose_words(words, first, step):
+            bank = psum.tile([P, BANK], F32, tag="bank")
+            for q in range(4):
+                nc.tensor.transpose(
+                    out=bank[:, q * P : (q + 1) * P],
+                    in_=words[:, first(q) : first(q) + step * (P - 1) + 1 : step],
+                    identity=ident[:],
+                )
+            return bank
+
+        def pair_up(copy, bank, grouped):
+            copy(
+                out=grouped.bitcast(F32).rearrange("p (a c u) -> p a c u", a=2, u=2),
+                in_=bank[:].rearrange("p (a u c) -> p a c u", a=2, u=2),
+            )
+
+        x_words = x_raw[:].bitcast(F32)
+        x_codes = keep.tile([P, PASSES * CHANNELS], U32, align_bytes=64)
+        x_scales = keep.tile([P, PASSES * CHANNELS], U8, align_bytes=64)
+        for g in range(PASSES):
+            x_grouped = work.tile([P, CHANNELS * PACK], BF16, align_bytes=64)
+            for half, copy in enumerate((nc.scalar.copy, nc.vector.tensor_copy)):
+                bank = transpose_words(
+                    x_words, lambda q: ((2 * g + q % 2) * GROUPS + 2 * half + q // 2) * P, 1
+                )
+                pair_up(copy, bank, x_grouped[:, half * 2 * BANK : (half + 1) * 2 * BANK])
+            cols = slice(g * CHANNELS, (g + 1) * CHANNELS)
+            nc.vector.quantize_mx(out=x_codes[:, cols].bitcast(FP8X4), scales=x_scales[:, cols], in_=x_grouped[:])
+
+        w_quantised = {}
+        agg_quantised = {}
+
+        def turn_weight(i):
+            w_words = w_raws[i][:].bitcast(F32)
+            w_grouped = work.tile([P, TILES * NODES], BF16, align_bytes=64)
+            w_codes = work.tile([P, TILES * BANK], U32, align_bytes=64)
+            w_scales = work.tile([P, TILES * BANK], U8, align_bytes=64)
+            for r in range(TILES):
+                for half in range(2):
+                    b = 2 * r + half
+                    bank = transpose_words(w_words, lambda q: (4 * b + q) * P, 1)
+                    pair_up(nc.scalar.copy, bank, w_grouped[:, b * 2 * BANK : (b + 1) * 2 * BANK])
+            for r in range(TILES):
+                cols = slice(r * BANK, (r + 1) * BANK)
+                nc.vector.quantize_mx(
+                    out=w_codes[:, cols].bitcast(FP8X4),
+                    scales=w_scales[:, cols],
+                    in_=w_grouped[:, r * NODES : (r + 1) * NODES],
+                )
+            w_quantised[i] = (w_codes, w_scales)
+
+        def aggregate(i):
+            w_codes, w_scales = w_quantised[i]
+            agg_grouped = work.tile([P, TILES * P * PACK], BF16, align_bytes=64)
+            agg_codes = work.tile([P, TILES * P], U32, align_bytes=64)
+            agg_scales = work.tile([P, TILES * P], U8, align_bytes=64)
+            for r in range(TILES):
+                agg_bank = psum.tile([P, BANK], F32, tag="bank")
+                for j in range(GROUPS):
+                    for g in range(PASSES):
+                        x_cols = slice(g * CHANNELS + j * P, g * CHANNELS + (j + 1) * P)
+                        w_cols = slice(r * BANK + g * P, r * BANK + (g + 1) * P)
+                        nc.tensor.matmul_mx(
+                            out=agg_bank[:, j * P : (j + 1) * P],
+                            lhsT=x_codes[:, x_cols].bitcast(FP8X4),
+                            lhsT_scale=x_scales[:, x_cols],
+                            rhs=w_codes[:, w_cols].bitcast(FP8X4),
+                            rhs_scale=w_scales[:, w_cols],
+                            start=(g == 0),
+                            stop=(g == PASSES - 1),
+                        )
+                nc.scalar.copy(
+                    out=agg_grouped[:, r * BANK : (r + 1) * BANK].rearrange("p (m j) -> p m j", j=GROUPS),
+                    in_=agg_bank[:].rearrange("p (j m) -> p m j", j=GROUPS),
+                )
+            nc.vector.quantize_mx(out=agg_codes[:].bitcast(FP8X4), scales=agg_scales[:], in_=agg_grouped[:])
+            agg_quantised[i] = (agg_codes, agg_scales)
+
+        def finish(i):
+            agg_codes, agg_scales = agg_quantised[i]
+            biased = work.tile([P, TILES * HIDDEN], F32)
+            result = work.tile([P, TILES * HIDDEN], F32)
+            for r in range(TILES):
+                out_bank = psum.tile([P, BANK], F32, tag="bank")
+                nc.tensor.matmul_mx(
+                    out=out_bank[:],
+                    lhsT=agg_codes[:, r * P : (r + 1) * P].bitcast(FP8X4),
+                    lhsT_scale=agg_scales[:, r * P : (r + 1) * P],
+                    rhs=w1_codes[:].bitcast(FP8X4),
+                    rhs_scale=w1_scales[:],
+                    start=True,
+                    stop=True,
+                )
+                nc.vector.tensor_tensor(
+                    out=biased[:, r * HIDDEN : (r + 1) * HIDDEN], in0=out_bank[:], in1=bias[:], op=ALU.add
+                )
+            nc.vector.scalar_tensor_tensor(
+                out=result[:], in0=biased[:], scalar=SLOPE, in1=biased[:], op0=ALU.mult, op1=ALU.max
+            )
+            nc.sync.dma_start(out=out_rounds[i], in_=result[:])
+
+        turn_weight(0)
+
+        w1_words = w1_raw[:].bitcast(F32)
+        w1_grouped = keep.tile([P, HIDDEN * PACK], BF16, align_bytes=64)
+        w1_codes = keep.tile([P, HIDDEN], U32, align_bytes=64)
+        w1_scales = keep.tile([P, HIDDEN], U8, align_bytes=64)
+        for half, copy in enumerate((nc.scalar.copy, nc.vector.tensor_copy)):
+            bank = transpose_words(w1_words, lambda q: (2 * half + q // 2) * (CHANNELS // 2) + q % 2, 2)
+            pair_up(copy, bank, w1_grouped[:, half * 2 * BANK : (half + 1) * 2 * BANK])
+        nc.vector.quantize_mx(out=w1_codes[:].bitcast(FP8X4), scales=w1_scales[:], in_=w1_grouped[:])
+
+        bias_bank = psum.tile([P, BANK], F32, tag="bank")
+        nc.tensor.matmul(out=bias_bank[:], lhsT=ones[:], rhs=bias_rows[:], start=True, stop=True)
+        bias = keep.tile([P, HIDDEN], F32)
+        nc.vector.tensor_copy(out=bias[:], in_=bias_bank[:])
+
+        for i in range(1, ROUNDS + 2):
+            if i < ROUNDS:
+                turn_weight(i)
+            if i - 1 < ROUNDS:
+                aggregate(i - 1)
+            if i >= 2:
+                finish(i - 2)

@@ -25,7 +25,7 @@ PASSES = NODES // K_PASS
 GROUPS = CHANNELS // P
 TILES = 2
 ROUNDS = NODES // (TILES * P)
-TILE_WORDS = NODES // 2
+TILE_CODES = PASSES * P
 
 FLOPS = 2 * NODES * NODES * CHANNELS + 2 * NODES * CHANNELS * HIDDEN
 
@@ -36,6 +36,7 @@ def tile_similargcn_pa_kernel(tc, x, weight, W1, b1, out):
         keep = ctx.enter_context(tc.tile_pool(name="keep", bufs=1))
         raw = ctx.enter_context(tc.tile_pool(name="raw", bufs=ROUNDS))
         work = ctx.enter_context(tc.tile_pool(name="work", bufs=3))
+        ends = ctx.enter_context(tc.tile_pool(name="ends", bufs=4))
         psum = ctx.enter_context(tc.psum_pool(name="psum", bufs=BANKS))
         ctx.enter_context(tc.manual_schedule())
 
@@ -95,30 +96,30 @@ def tile_similargcn_pa_kernel(tc, x, weight, W1, b1, out):
             cols = slice(g * CHANNELS, (g + 1) * CHANNELS)
             nc.vector.quantize_mx(out=x_codes[:, cols].bitcast(FP8X4), scales=x_scales[:, cols], in_=x_grouped[:])
 
-        w_quantised = {}
-        agg_quantised = {}
+        w_tiles = {}
+        agg_tiles = {}
 
         def turn_weight(i):
             w_words = w_raws[i][:].bitcast(F32)
             w_grouped = work.tile([P, TILES * NODES], BF16, align_bytes=64)
-            w_codes = work.tile([P, TILES * BANK], U32, align_bytes=64)
-            w_scales = work.tile([P, TILES * BANK], U8, align_bytes=64)
-            for r in range(TILES):
-                for half in range(2):
-                    b = 2 * r + half
-                    bank = transpose_words(w_words, lambda q: (4 * b + q) * P, 1)
-                    pair_up(nc.scalar.copy, bank, w_grouped[:, b * 2 * BANK : (b + 1) * 2 * BANK])
-            for r in range(TILES):
-                cols = slice(r * BANK, (r + 1) * BANK)
-                nc.vector.quantize_mx(
-                    out=w_codes[:, cols].bitcast(FP8X4),
-                    scales=w_scales[:, cols],
-                    in_=w_grouped[:, r * NODES : (r + 1) * NODES],
-                )
-            w_quantised[i] = (w_codes, w_scales)
+            w_codes = work.tile([P, TILES * TILE_CODES], U32, align_bytes=64)
+            w_scales = work.tile([P, TILES * TILE_CODES], U8, align_bytes=64)
+            for b in range(2 * TILES):
+                bank = transpose_words(w_words, lambda q: (4 * b + q) * P, 1)
+                pair_up(nc.scalar.copy, bank, w_grouped[:, b * 2 * BANK : (b + 1) * 2 * BANK])
+            w_tiles[i] = (w_grouped, w_codes, w_scales)
+
+        def quantise_weight(i, r):
+            w_grouped, w_codes, w_scales = w_tiles[i]
+            cols = slice(r * TILE_CODES, (r + 1) * TILE_CODES)
+            nc.vector.quantize_mx(
+                out=w_codes[:, cols].bitcast(FP8X4),
+                scales=w_scales[:, cols],
+                in_=w_grouped[:, r * NODES : (r + 1) * NODES],
+            )
 
         def aggregate(i):
-            w_codes, w_scales = w_quantised[i]
+            w_grouped, w_codes, w_scales = w_tiles[i]
             agg_grouped = work.tile([P, TILES * P * PACK], BF16, align_bytes=64)
             agg_codes = work.tile([P, TILES * P], U32, align_bytes=64)
             agg_scales = work.tile([P, TILES * P], U8, align_bytes=64)
@@ -127,7 +128,7 @@ def tile_similargcn_pa_kernel(tc, x, weight, W1, b1, out):
                 for j in range(GROUPS):
                     for g in range(PASSES):
                         x_cols = slice(g * CHANNELS + j * P, g * CHANNELS + (j + 1) * P)
-                        w_cols = slice(r * BANK + g * P, r * BANK + (g + 1) * P)
+                        w_cols = slice(r * TILE_CODES + g * P, r * TILE_CODES + (g + 1) * P)
                         nc.tensor.matmul_mx(
                             out=agg_bank[:, j * P : (j + 1) * P],
                             lhsT=x_codes[:, x_cols].bitcast(FP8X4),
@@ -137,37 +138,44 @@ def tile_similargcn_pa_kernel(tc, x, weight, W1, b1, out):
                             start=(g == 0),
                             stop=(g == PASSES - 1),
                         )
+                values = agg_grouped[:, r * P * PACK : (r + 1) * P * PACK]
                 nc.scalar.copy(
-                    out=agg_grouped[:, r * BANK : (r + 1) * BANK].rearrange("p (m j) -> p m j", j=GROUPS),
+                    out=values.rearrange("p (m j) -> p m j", j=GROUPS),
                     in_=agg_bank[:].rearrange("p (j m) -> p m j", j=GROUPS),
                 )
-            nc.vector.quantize_mx(out=agg_codes[:].bitcast(FP8X4), scales=agg_scales[:], in_=agg_grouped[:])
-            agg_quantised[i] = (agg_codes, agg_scales)
+                nc.vector.quantize_mx(
+                    out=agg_codes[:, r * P : (r + 1) * P].bitcast(FP8X4),
+                    scales=agg_scales[:, r * P : (r + 1) * P],
+                    in_=values,
+                )
+            agg_tiles[i] = (agg_codes, agg_scales)
 
-        def finish(i):
-            agg_codes, agg_scales = agg_quantised[i]
-            biased = work.tile([P, TILES * HIDDEN], F32)
-            result = work.tile([P, TILES * HIDDEN], F32)
-            for r in range(TILES):
-                out_bank = psum.tile([P, BANK], F32, tag="bank")
-                nc.tensor.matmul_mx(
-                    out=out_bank[:],
-                    lhsT=agg_codes[:, r * P : (r + 1) * P].bitcast(FP8X4),
-                    lhsT_scale=agg_scales[:, r * P : (r + 1) * P],
-                    rhs=w1_codes[:].bitcast(FP8X4),
-                    rhs_scale=w1_scales[:],
-                    start=True,
-                    stop=True,
-                )
-                nc.vector.tensor_tensor(
-                    out=biased[:, r * HIDDEN : (r + 1) * HIDDEN], in0=out_bank[:], in1=bias[:], op=ALU.add
-                )
+        def project(i, r):
+            agg_codes, agg_scales = agg_tiles[i]
+            out_bank = psum.tile([P, BANK], F32, tag="bank")
+            nc.tensor.matmul_mx(
+                out=out_bank[:],
+                lhsT=agg_codes[:, r * P : (r + 1) * P].bitcast(FP8X4),
+                lhsT_scale=agg_scales[:, r * P : (r + 1) * P],
+                rhs=w1_codes[:].bitcast(FP8X4),
+                rhs_scale=w1_scales[:],
+                start=True,
+                stop=True,
+            )
+            biased = ends.tile([P, HIDDEN], F32)
+            nc.vector.tensor_tensor(out=biased[:], in0=out_bank[:], in1=bias[:], op=ALU.add)
+            return biased
+
+        def leaky_store(biased, i, r):
+            result = ends.tile([P, HIDDEN], F32)
             nc.vector.scalar_tensor_tensor(
                 out=result[:], in0=biased[:], scalar=SLOPE, in1=biased[:], op0=ALU.mult, op1=ALU.max
             )
-            nc.sync.dma_start(out=out_rounds[i], in_=result[:])
+            nc.sync.dma_start(out=out_rounds[i][:, r * HIDDEN : (r + 1) * HIDDEN], in_=result[:])
 
         turn_weight(0)
+        for r in range(TILES):
+            quantise_weight(0, r)
 
         w1_words = w1_raw[:].bitcast(F32)
         w1_grouped = keep.tile([P, HIDDEN * PACK], BF16, align_bytes=64)
@@ -183,10 +191,17 @@ def tile_similargcn_pa_kernel(tc, x, weight, W1, b1, out):
         bias = keep.tile([P, HIDDEN], F32)
         nc.vector.tensor_copy(out=bias[:], in_=bias_bank[:])
 
-        for i in range(1, ROUNDS + 2):
+        aggregate(0)
+        turn_weight(1)
+        for r in range(TILES):
+            quantise_weight(1, r)
+        for i in range(2, ROUNDS + 2):
             if i < ROUNDS:
                 turn_weight(i)
+            for r in range(TILES):
+                biased = project(i - 2, r)
+                if i < ROUNDS:
+                    quantise_weight(i, r)
+                leaky_store(biased, i - 2, r)
             if i - 1 < ROUNDS:
                 aggregate(i - 1)
-            if i >= 2:
-                finish(i - 2)

@@ -118,12 +118,15 @@ def tile_similargcn_pa_kernel(tc, x, weight, W1, b1, out):
                 in_=w_grouped[:, r * NODES : (r + 1) * NODES],
             )
 
-        def aggregate(i):
+        def aggregate(i, tiles):
             w_grouped, w_codes, w_scales = w_tiles[i]
-            agg_grouped = work.tile([P, TILES * P * PACK], BF16, align_bytes=64)
-            agg_codes = work.tile([P, TILES * P], U32, align_bytes=64)
-            agg_scales = work.tile([P, TILES * P], U8, align_bytes=64)
-            for r in range(TILES):
+            if i not in agg_tiles:
+                agg_grouped = work.tile([P, TILES * P * PACK], BF16, align_bytes=64)
+                agg_codes = work.tile([P, TILES * P], U32, align_bytes=64)
+                agg_scales = work.tile([P, TILES * P], U8, align_bytes=64)
+                agg_tiles[i] = (agg_grouped, agg_codes, agg_scales)
+            agg_grouped, agg_codes, agg_scales = agg_tiles[i]
+            for r in tiles:
                 agg_bank = psum.tile([P, BANK], F32, tag="bank")
                 for j in range(GROUPS):
                     for g in range(PASSES):
@@ -148,10 +151,9 @@ def tile_similargcn_pa_kernel(tc, x, weight, W1, b1, out):
                     scales=agg_scales[:, r * P : (r + 1) * P],
                     in_=values,
                 )
-            agg_tiles[i] = (agg_codes, agg_scales)
 
         def project(i, r):
-            agg_codes, agg_scales = agg_tiles[i]
+            agg_grouped, agg_codes, agg_scales = agg_tiles[i]
             out_bank = psum.tile([P, BANK], F32, tag="bank")
             nc.tensor.matmul_mx(
                 out=out_bank[:],
@@ -191,17 +193,19 @@ def tile_similargcn_pa_kernel(tc, x, weight, W1, b1, out):
         bias = keep.tile([P, HIDDEN], F32)
         nc.vector.tensor_copy(out=bias[:], in_=bias_bank[:])
 
-        aggregate(0)
+        aggregate(0, (0, 1))
         turn_weight(1)
         for r in range(TILES):
             quantise_weight(1, r)
         for i in range(2, ROUNDS + 2):
             if i < ROUNDS:
                 turn_weight(i)
-            for r in range(TILES):
-                biased = project(i - 2, r)
-                if i < ROUNDS:
+                for r in range(TILES):
                     quantise_weight(i, r)
-                leaky_store(biased, i - 2, r)
             if i - 1 < ROUNDS:
-                aggregate(i - 1)
+                aggregate(i - 1, (0,))
+            sums = [project(i - 2, r) for r in range(TILES)]
+            for r in range(TILES):
+                leaky_store(sums[r], i - 2, r)
+            if i - 1 < ROUNDS:
+                aggregate(i - 1, (1,))

from contextlib import ExitStack

import concourse.mybir as mybir
from concourse.masks import make_identity

F32 = mybir.dt.float32
BF16 = mybir.dt.bfloat16
U32 = mybir.dt.uint32
U8 = mybir.dt.uint8
FP8X4 = mybir.dt.float8_e4m3fn_x4
ALU = mybir.AluOpType

P = 128
PACK = 4
K_PASS = P * PACK
BANK = 512
BANKS = 8

SAMPLES, CHANNELS, PIXELS = 8, 512, 256
NODES = SAMPLES * PIXELS
HIDDEN = 512
SLOPE = 0.01

PASSES = NODES // K_PASS
GROUPS = CHANNELS // P
TILES = 2
ROUNDS = NODES // (TILES * P)
TILE_CODES = PASSES * P

FLOPS = 2 * NODES * NODES * CHANNELS + 2 * NODES * CHANNELS * HIDDEN


def tile_similargcn_pa_kernel(tc, x, weight, W1, b1, out):
    nc = tc.nc
    with ExitStack() as ctx:
        keep = ctx.enter_context(tc.tile_pool(name="keep", bufs=1))
        raw = ctx.enter_context(tc.tile_pool(name="raw", bufs=ROUNDS))
        work = ctx.enter_context(tc.tile_pool(name="work", bufs=3))
        ends = ctx.enter_context(tc.tile_pool(name="ends", bufs=4))
        psum = ctx.enter_context(tc.psum_pool(name="psum", bufs=BANKS))
        ctx.enter_context(tc.manual_schedule())

        ident = keep.tile([P, P], F32)
        make_identity(nc, ident[:])
        ones = keep.tile([P, P], BF16)
        nc.gpsimd.memset(ones[:], 1.0)
        bias_rows = keep.tile([P, HIDDEN], BF16)
        nc.gpsimd.memset(bias_rows[:], 0.0)

        x_view = x.rearrange("n (p j) h w -> p n (j h w)", j=GROUPS)
        x_raw = keep.tile([P, SAMPLES * GROUPS * PIXELS], BF16)
        x_raw_by_sample = x_raw[:].rearrange("p (n f) -> p n f", n=SAMPLES)
        for g in range(PASSES):
            nc.sync.dma_start(out=x_raw_by_sample[:, 2 * g : 2 * g + 2, :], in_=x_view[:, 2 * g : 2 * g + 2, :])
        weight_rounds = weight.rearrange("(i p r) k -> i p (r k)", p=P, r=TILES)
        out_rounds = out.rearrange("(i p r) h -> i p (r h)", p=P, r=TILES)
        w1_raw = keep.tile([P, GROUPS * CHANNELS], BF16)
        w_raws = []
        for i in range(ROUNDS):
            w_raw = raw.tile([P, TILES * NODES], BF16)
            nc.sync.dma_start(out=w_raw[:], in_=weight_rounds[i])
            w_raws.append(w_raw)
            if i == 0:
                nc.sync.dma_start(
                    out=w1_raw[:].rearrange("p (a c) -> p a c", a=GROUPS),
                    in_=W1.rearrange("(a p) c -> p a c", p=P),
                )
                nc.sync.dma_start(out=bias_rows[0:1, :], in_=b1.rearrange("(o h) -> o h", o=1))

        def transpose_words(words, first, step):
            bank = psum.tile([P, BANK], F32, tag="bank")
            for q in range(4):
                nc.tensor.transpose(
                    out=bank[:, q * P : (q + 1) * P],
                    in_=words[:, first(q) : first(q) + step * (P - 1) + 1 : step],
                    identity=ident[:],
                )
            return bank

        def pair_up(copy, bank, grouped):
            copy(
                out=grouped.bitcast(F32).rearrange("p (a c u) -> p a c u", a=2, u=2),
                in_=bank[:].rearrange("p (a u c) -> p a c u", a=2, u=2),
            )

        x_words = x_raw[:].bitcast(F32)
        x_codes = keep.tile([P, PASSES * CHANNELS], U32, align_bytes=64)
        x_scales = keep.tile([P, PASSES * CHANNELS], U8, align_bytes=64)
        for g in range(PASSES):
            x_grouped = work.tile([P, CHANNELS * PACK], BF16, align_bytes=64)
            for half, copy in enumerate((nc.scalar.copy, nc.vector.tensor_copy)):
                bank = transpose_words(
                    x_words, lambda q: ((2 * g + q % 2) * GROUPS + 2 * half + q // 2) * P, 1
                )
                pair_up(copy, bank, x_grouped[:, half * 2 * BANK : (half + 1) * 2 * BANK])
            cols = slice(g * CHANNELS, (g + 1) * CHANNELS)
            nc.vector.quantize_mx(out=x_codes[:, cols].bitcast(FP8X4), scales=x_scales[:, cols], in_=x_grouped[:])

        w_tiles = {}
        agg_tiles = {}

        def turn_weight(i):
            w_words = w_raws[i][:].bitcast(F32)
            w_grouped = work.tile([P, TILES * NODES], BF16, align_bytes=64)
            w_codes = work.tile([P, TILES * TILE_CODES], U32, align_bytes=64)
            w_scales = work.tile([P, TILES * TILE_CODES], U8, align_bytes=64)
            for b in range(2 * TILES):
                bank = transpose_words(w_words, lambda q: (4 * b + q) * P, 1)
                pair_up(nc.scalar.copy, bank, w_grouped[:, b * 2 * BANK : (b + 1) * 2 * BANK])
            w_tiles[i] = (w_grouped, w_codes, w_scales)

        def quantise_weight(i, r):
            w_grouped, w_codes, w_scales = w_tiles[i]
            cols = slice(r * TILE_CODES, (r + 1) * TILE_CODES)
            nc.vector.quantize_mx(
                out=w_codes[:, cols].bitcast(FP8X4),
                scales=w_scales[:, cols],
                in_=w_grouped[:, r * NODES : (r + 1) * NODES],
            )

        def aggregate(i, tiles):
            w_grouped, w_codes, w_scales = w_tiles[i]
            if i not in agg_tiles:
                agg_grouped = work.tile([P, TILES * P * PACK], BF16, align_bytes=64)
                agg_codes = work.tile([P, TILES * P], U32, align_bytes=64)
                agg_scales = work.tile([P, TILES * P], U8, align_bytes=64)
                agg_tiles[i] = (agg_grouped, agg_codes, agg_scales)
            agg_grouped, agg_codes, agg_scales = agg_tiles[i]
            for r in tiles:
                agg_bank = psum.tile([P, BANK], F32, tag="bank")
                for j in range(GROUPS):
                    for g in range(PASSES):
                        x_cols = slice(g * CHANNELS + j * P, g * CHANNELS + (j + 1) * P)
                        w_cols = slice(r * TILE_CODES + g * P, r * TILE_CODES + (g + 1) * P)
                        nc.tensor.matmul_mx(
                            out=agg_bank[:, j * P : (j + 1) * P],
                            lhsT=x_codes[:, x_cols].bitcast(FP8X4),
                            lhsT_scale=x_scales[:, x_cols],
                            rhs=w_codes[:, w_cols].bitcast(FP8X4),
                            rhs_scale=w_scales[:, w_cols],
                            start=(g == 0),
                            stop=(g == PASSES - 1),
                        )
                values = agg_grouped[:, r * P * PACK : (r + 1) * P * PACK]
                nc.scalar.copy(
                    out=values.rearrange("p (m j) -> p m j", j=GROUPS),
                    in_=agg_bank[:].rearrange("p (j m) -> p m j", j=GROUPS),
                )
                nc.vector.quantize_mx(
                    out=agg_codes[:, r * P : (r + 1) * P].bitcast(FP8X4),
                    scales=agg_scales[:, r * P : (r + 1) * P],
                    in_=values,
                )

        def project(i, r):
            agg_grouped, agg_codes, agg_scales = agg_tiles[i]
            out_bank = psum.tile([P, BANK], F32, tag="bank")
            nc.tensor.matmul_mx(
                out=out_bank[:],
                lhsT=agg_codes[:, r * P : (r + 1) * P].bitcast(FP8X4),
                lhsT_scale=agg_scales[:, r * P : (r + 1) * P],
                rhs=w1_codes[:].bitcast(FP8X4),
                rhs_scale=w1_scales[:],
                start=True,
                stop=True,
            )
            biased = ends.tile([P, HIDDEN], F32)
            nc.vector.tensor_tensor(out=biased[:], in0=out_bank[:], in1=bias[:], op=ALU.add)
            return biased

        def leaky_store(biased, i, r):
            result = ends.tile([P, HIDDEN], F32)
            nc.vector.scalar_tensor_tensor(
                out=result[:], in0=biased[:], scalar=SLOPE, in1=biased[:], op0=ALU.mult, op1=ALU.max
            )
            nc.sync.dma_start(out=out_rounds[i][:, r * HIDDEN : (r + 1) * HIDDEN], in_=result[:])

        turn_weight(0)
        for r in range(TILES):
            quantise_weight(0, r)

        w1_words = w1_raw[:].bitcast(F32)
        w1_grouped = keep.tile([P, HIDDEN * PACK], BF16, align_bytes=64)
        w1_codes = keep.tile([P, HIDDEN], U32, align_bytes=64)
        w1_scales = keep.tile([P, HIDDEN], U8, align_bytes=64)
        for half, copy in enumerate((nc.scalar.copy, nc.vector.tensor_copy)):
            bank = transpose_words(w1_words, lambda q: (2 * half + q // 2) * (CHANNELS // 2) + q % 2, 2)
            pair_up(copy, bank, w1_grouped[:, half * 2 * BANK : (half + 1) * 2 * BANK])
        nc.vector.quantize_mx(out=w1_codes[:].bitcast(FP8X4), scales=w1_scales[:], in_=w1_grouped[:])

        bias_bank = psum.tile([P, BANK], F32, tag="bank")
        nc.tensor.matmul(out=bias_bank[:], lhsT=ones[:], rhs=bias_rows[:], start=True, stop=True)
        bias = keep.tile([P, HIDDEN], F32)
        nc.vector.tensor_copy(out=bias[:], in_=bias_bank[:])

        aggregate(0, (0, 1))
        turn_weight(1)
        for r in range(TILES):
            quantise_weight(1, r)
        for i in range(2, ROUNDS + 2):
            if i < ROUNDS:
                turn_weight(i)
                for r in range(TILES):
                    quantise_weight(i, r)
            if i - 1 < ROUNDS:
                aggregate(i - 1, (0,))
            sums = [project(i - 2, r) for r in range(TILES)]
            for r in range(TILES):
                leaky_store(sums[r], i - 2, r)
            if i - 1 < ROUNDS:
                aggregate(i - 1, (1,))
